import numpy as np
import ml_dtypes

BF16 = ml_dtypes.bfloat16


def bf(x):
    return np.asarray(x, np.float32).astype(BF16)


def f32(x):
    return np.asarray(x, np.float32)


def f64(x):
    return np.asarray(x).astype(np.float64)


def striped(idx):
    return np.tile(idx.reshape(-1, 16).T, (8, 1))


C, H, D, K, S, N = 1024, 128, 8, 1024, 512, 128
EPS = 1e-6


def setup_inputs():
    return {"base": f32(np.random.standard_normal((C, S))), "x": bf(np.random.standard_normal((K, N))), "w": bf(np.random.standard_normal((K, C)) / np.sqrt(K)), "offs": striped(np.random.permutation(S)[:N])}


def reference(base, x, w, offs):
    idx = offs[:16].T.reshape(-1)
    raw = f64(w).T @ f64(x)
    r3 = raw.reshape(D, H, N)
    rstd = 1.0 / np.sqrt(np.mean(r3 * r3, axis=0) + EPS)
    out = f64(base).copy()
    out[:, idx] = (r3 * rstd[None, :, :]).reshape(C, N)
    return out

@@ -1,0 +1,65 @@
+import concourse.mybir as mybir
+
+BF16, F32, U16 = mybir.dt.bfloat16, mybir.dt.float32, mybir.dt.uint16
+ACT = mybir.ActivationFunctionType
+ALU = mybir.AluOpType
+
+P = 128
+C, S = 1024, 512
+K, N = 1024, 128
+D = C // P
+KB = K // P
+EPS = 1e-6
+FLOPS = 2 * K * C * N
+
+
+def tile_gemma4attention_kernel(tc, base, x, w, offs, out):
+    nc = tc.nc
+    x_rows = x.rearrange("(p b) j -> p b j", b=KB)
+    w_rows = w.rearrange("(p b) c -> p b c", b=KB)
+    base_blocks = base.rearrange("(d p) s -> d p s", p=P)
+    out_blocks = out.rearrange("(d p) s -> d p s", p=P)
+
+    with (
+        tc.tile_pool(name="held", bufs=1) as held,
+        tc.psum_pool(name="psum", bufs=1) as psum,
+    ):
+        offsets = held.tile([P, N // 16], U16, name="offsets")
+        nc.sync.dma_start(offsets[:], offs)
+        x_sb = held.tile([P, KB, N], BF16, name="x_sb")
+        nc.sync.dma_start(x_sb[:], x_rows)
+
+        queues = (nc.sync, nc.scalar)
+        w_sb = [held.tile([P, C], BF16, name=f"w_sb{b}") for b in range(KB)]
+        for b in range(KB):
+            queues[b % 2].dma_start(w_sb[b][:], w_rows[:, b, :])
+        windows = [held.tile([P, S], F32, name=f"window{d}") for d in range(D)]
+        for d in range(D):
+            queues[d % 2].dma_start(windows[d][:], base_blocks[d])
+
+        raw = [psum.tile([P, N], F32, name=f"raw{d}") for d in range(D)]
+        for b in range(KB):
+            for d in range(D):
+                nc.tensor.matmul(
+                    raw[d][:], w_sb[b][:, d * P : (d + 1) * P], x_sb[:, b, :],
+                    start=(b == 0), stop=(b == KB - 1),
+                )
+
+        raw_sb = [held.tile([P, N], F32, name=f"raw_sb{d}") for d in range(D)]
+        sum_sq = held.tile([P, N], F32, name="sum_sq")
+        for d in range(D):
+            nc.vector.tensor_copy(raw_sb[d][:], raw[d][:])
+            if d == 0:
+                nc.scalar.activation(sum_sq[:], raw_sb[d][:], ACT.Square)
+            else:
+                square = held.tile([P, N], F32, name=f"square{d}")
+                nc.scalar.activation(square[:], raw_sb[d][:], ACT.Square)
+                nc.vector.tensor_add(sum_sq[:], sum_sq[:], square[:])
+        rms = held.tile([P, N], F32, name="rms")
+        nc.scalar.activation(rms[:], sum_sq[:], ACT.Sqrt, bias=EPS, scale=1.0 / D)
+        r = held.tile([P, N], F32, name="r")
+        nc.vector.reciprocal(r[:], rms[:])
+
+        for d in range(D):
+            nc.vector.tensor_tensor(windows[d][:].indirect(offsets[:]), raw_sb[d][:], r[:], ALU.mult)
+            queues[d % 2].dma_start(out_blocks[d], windows[d][:])

@@ -11,6 +11,7 @@ D = C // P
 KB = K // P
 EPS = 1e-6
 FLOPS = 2 * K * C * N
+KB_STREAMED = 6
 
 
 def tile_gemma4attention_kernel(tc, base, x, w, offs, out):
@@ -24,37 +25,45 @@ def tile_gemma4attention_kernel(tc, base, x, w, offs, out):
         tc.tile_pool(name="held", bufs=1) as held,
         tc.psum_pool(name="psum", bufs=1) as psum,
     ):
-        offsets = held.tile([P, N // 16], U16, name="offsets")
-        nc.sync.dma_start(offsets[:], offs)
+        queues = (nc.scalar, nc.sync)
         x_sb = held.tile([P, KB, N], BF16, name="x_sb")
         nc.sync.dma_start(x_sb[:], x_rows)
-
-        queues = (nc.sync, nc.scalar)
         w_sb = [held.tile([P, C], BF16, name=f"w_sb{b}") for b in range(KB)]
         for b in range(KB):
             queues[b % 2].dma_start(w_sb[b][:], w_rows[:, b, :])
+        offsets = held.tile([P, N // 16], U16, name="offsets")
+        nc.sync.dma_start(offsets[:], offs)
         windows = [held.tile([P, S], F32, name=f"window{d}") for d in range(D)]
         for d in range(D):
-            queues[d % 2].dma_start(windows[d][:], base_blocks[d])
+            nc.sync.dma_start(windows[d][:], base_blocks[d])
+
+        warm = held.tile([P, 1], F32, name="warm")
+        nc.vector.memset(warm[:], 1.0)
+        nc.scalar.activation(warm[:], warm[:], ACT.Sqrt)
 
         raw = [psum.tile([P, N], F32, name=f"raw{d}") for d in range(D)]
-        for b in range(KB):
-            for d in range(D):
-                nc.tensor.matmul(
-                    raw[d][:], w_sb[b][:, d * P : (d + 1) * P], x_sb[:, b, :],
-                    start=(b == 0), stop=(b == KB - 1),
-                )
-
         raw_sb = [held.tile([P, N], F32, name=f"raw_sb{d}") for d in range(D)]
         sum_sq = held.tile([P, N], F32, name="sum_sq")
+
+        def multiply(b, d):
+            nc.tensor.matmul(
+                raw[d][:], w_sb[b][:, d * P : (d + 1) * P], x_sb[:, b, :],
+                start=(b == 0), stop=(b == KB - 1),
+            )
+
+        for b in range(KB_STREAMED):
+            for d in range(D):
+                multiply(b, d)
         for d in range(D):
-            nc.vector.tensor_copy(raw_sb[d][:], raw[d][:])
+            for b in range(KB_STREAMED, KB):
+                multiply(b, d)
             if d == 0:
-                nc.scalar.activation(sum_sq[:], raw_sb[d][:], ACT.Square)
+                nc.scalar.activation(sum_sq[:], raw[d][:], ACT.Square)
             else:
                 square = held.tile([P, N], F32, name=f"square{d}")
-                nc.scalar.activation(square[:], raw_sb[d][:], ACT.Square)
+                nc.scalar.activation(square[:], raw[d][:], ACT.Square)
                 nc.vector.tensor_add(sum_sq[:], sum_sq[:], square[:])
+            nc.vector.tensor_copy(raw_sb[d][:], raw[d][:])
         rms = held.tile([P, N], F32, name="rms")
         nc.scalar.activation(rms[:], sum_sq[:], ACT.Sqrt, bias=EPS, scale=1.0 / D)
         r = held.tile([P, N], F32, name="r")

@@ -12,6 +12,7 @@ KB = K // P
 EPS = 1e-6
 FLOPS = 2 * K * C * N
 KB_STREAMED = 6
+N_WARM = 18
 
 
 def tile_gemma4attention_kernel(tc, base, x, w, offs, out):
@@ -37,13 +38,16 @@ def tile_gemma4attention_kernel(tc, base, x, w, offs, out):
         for d in range(D):
             nc.sync.dma_start(windows[d][:], base_blocks[d])
 
-        warm = held.tile([P, 1], F32, name="warm")
-        nc.vector.memset(warm[:], 1.0)
-        nc.scalar.activation(warm[:], warm[:], ACT.Sqrt)
-
         raw = [psum.tile([P, N], F32, name=f"raw{d}") for d in range(D)]
         raw_sb = [held.tile([P, N], F32, name=f"raw_sb{d}") for d in range(D)]
-        sum_sq = held.tile([P, N], F32, name="sum_sq")
+
+        zeros = held.tile([P, N], BF16, name="zeros")
+        nc.gpsimd.memset(zeros[:], 0.0)
+        for i in range(N_WARM):
+            nc.tensor.matmul(raw[D - 1][:], zeros[:], zeros[:], start=True, stop=True)
+        one = held.tile([P, 1], F32, name="one")
+        nc.vector.memset(one[:], 1.0)
+        nc.scalar.activation(one[:], one[:], ACT.Sqrt)
 
         def multiply(b, d):
             nc.tensor.matmul(
@@ -54,18 +58,20 @@ def tile_gemma4attention_kernel(tc, base, x, w, offs, out):
         for b in range(KB_STREAMED):
             for d in range(D):
                 multiply(b, d)
+        sum_sq = [held.tile([P, N], F32, name=f"sum_sq{i}") for i in range(2)]
         for d in range(D):
             for b in range(KB_STREAMED, KB):
                 multiply(b, d)
-            if d == 0:
-                nc.scalar.activation(sum_sq[:], raw[d][:], ACT.Square)
+            if d < 2:
+                nc.scalar.activation(sum_sq[d][:], raw[d][:], ACT.Square)
             else:
                 square = held.tile([P, N], F32, name=f"square{d}")
                 nc.scalar.activation(square[:], raw[d][:], ACT.Square)
-                nc.vector.tensor_add(sum_sq[:], sum_sq[:], square[:])
+                nc.vector.tensor_add(sum_sq[d % 2][:], sum_sq[d % 2][:], square[:])
             nc.vector.tensor_copy(raw_sb[d][:], raw[d][:])
+        nc.vector.tensor_add(sum_sq[0][:], sum_sq[0][:], sum_sq[1][:])
         rms = held.tile([P, N], F32, name="rms")
-        nc.scalar.activation(rms[:], sum_sq[:], ACT.Sqrt, bias=EPS, scale=1.0 / D)
+        nc.scalar.activation(rms[:], sum_sq[0][:], ACT.Sqrt, bias=EPS, scale=1.0 / D)
         r = held.tile([P, N], F32, name="r")
         nc.vector.reciprocal(r[:], rms[:])
 

@@ -47,7 +47,7 @@ def tile_gemma4attention_kernel(tc, base, x, w, offs, out):
             nc.tensor.matmul(raw[D - 1][:], zeros[:], zeros[:], start=True, stop=True)
         one = held.tile([P, 1], F32, name="one")
         nc.vector.memset(one[:], 1.0)
-        nc.scalar.activation(one[:], one[:], ACT.Sqrt)
+        nc.scalar.activation(one[:], one[:], ACT.Abs_reciprocal_sqrt)
 
         def multiply(b, d):
             nc.tensor.matmul(
@@ -70,10 +70,8 @@ def tile_gemma4attention_kernel(tc, base, x, w, offs, out):
                 nc.vector.tensor_add(sum_sq[d % 2][:], sum_sq[d % 2][:], square[:])
             nc.vector.tensor_copy(raw_sb[d][:], raw[d][:])
         nc.vector.tensor_add(sum_sq[0][:], sum_sq[0][:], sum_sq[1][:])
-        rms = held.tile([P, N], F32, name="rms")
-        nc.scalar.activation(rms[:], sum_sq[0][:], ACT.Sqrt, bias=EPS, scale=1.0 / D)
         r = held.tile([P, N], F32, name="r")
-        nc.vector.reciprocal(r[:], rms[:])
+        nc.scalar.activation(r[:], sum_sq[0][:], ACT.Abs_reciprocal_sqrt, bias=EPS, scale=1.0 / D)
 
         for d in range(D):
             nc.vector.tensor_tensor(windows[d][:].indirect(offsets[:]), raw_sb[d][:], r[:], ALU.mult)

@@ -12,6 +12,8 @@ KB = K // P
 EPS = 1e-6
 FLOPS = 2 * K * C * N
 KB_STREAMED = 6
+KB_LAST = KB - KB_STREAMED
+D_PIECE = 2
 N_WARM = 18
 
 
@@ -26,12 +28,18 @@ def tile_gemma4attention_kernel(tc, base, x, w, offs, out):
         tc.tile_pool(name="held", bufs=1) as held,
         tc.psum_pool(name="psum", bufs=1) as psum,
     ):
-        queues = (nc.scalar, nc.sync)
         x_sb = held.tile([P, KB, N], BF16, name="x_sb")
         nc.sync.dma_start(x_sb[:], x_rows)
-        w_sb = [held.tile([P, C], BF16, name=f"w_sb{b}") for b in range(KB)]
-        for b in range(KB):
-            queues[b % 2].dma_start(w_sb[b][:], w_rows[:, b, :])
+        w_whole = [held.tile([P, C], BF16, name=f"w_whole{b}") for b in range(KB_STREAMED)]
+        for b in range(KB_STREAMED):
+            nc.sync.dma_start(w_whole[b][:], w_rows[:, b, :])
+        w_piece = [
+            held.tile([P, KB_LAST, D_PIECE * P], BF16, name=f"w_piece{g}") for g in range(D // D_PIECE)
+        ]
+        for g in range(D // D_PIECE):
+            nc.sync.dma_start(
+                w_piece[g][:], w_rows[:, KB_STREAMED:, g * D_PIECE * P : (g + 1) * D_PIECE * P]
+            )
         offsets = held.tile([P, N // 16], U16, name="offsets")
         nc.sync.dma_start(offsets[:], offs)
         windows = [held.tile([P, S], F32, name=f"window{d}") for d in range(D)]
@@ -50,10 +58,12 @@ def tile_gemma4attention_kernel(tc, base, x, w, offs, out):
         nc.scalar.activation(one[:], one[:], ACT.Abs_reciprocal_sqrt)
 
         def multiply(b, d):
-            nc.tensor.matmul(
-                raw[d][:], w_sb[b][:, d * P : (d + 1) * P], x_sb[:, b, :],
-                start=(b == 0), stop=(b == KB - 1),
-            )
+            if b < KB_STREAMED:
+                weights = w_whole[b][:, d * P : (d + 1) * P]
+            else:
+                g, i = divmod(d, D_PIECE)
+                weights = w_piece[g][:, b - KB_STREAMED, i * P : (i + 1) * P]
+            nc.tensor.matmul(raw[d][:], weights, x_sb[:, b, :], start=(b == 0), stop=(b == KB - 1))
 
         for b in range(KB_STREAMED):
             for d in range(D):
@@ -73,6 +83,7 @@ def tile_gemma4attention_kernel(tc, base, x, w, offs, out):
         r = held.tile([P, N], F32, name="r")
         nc.scalar.activation(r[:], sum_sq[0][:], ACT.Abs_reciprocal_sqrt, bias=EPS, scale=1.0 / D)
 
+        queues = (nc.scalar, nc.sync)
         for d in range(D):
             nc.vector.tensor_tensor(windows[d][:].indirect(offsets[:]), raw_sb[d][:], r[:], ALU.mult)
             queues[d % 2].dma_start(out_blocks[d], windows[d][:])

@@ -11,9 +11,6 @@ D = C // P
 KB = K // P
 EPS = 1e-6
 FLOPS = 2 * K * C * N
-KB_STREAMED = 6
-KB_LAST = KB - KB_STREAMED
-D_PIECE = 2
 N_WARM = 18
 
 
@@ -30,16 +27,9 @@ def tile_gemma4attention_kernel(tc, base, x, w, offs, out):
     ):
         x_sb = held.tile([P, KB, N], BF16, name="x_sb")
         nc.sync.dma_start(x_sb[:], x_rows)
-        w_whole = [held.tile([P, C], BF16, name=f"w_whole{b}") for b in range(KB_STREAMED)]
-        for b in range(KB_STREAMED):
+        w_whole = [held.tile([P, C], BF16, name=f"w_whole{b}") for b in range(KB)]
+        for b in range(KB):
             nc.sync.dma_start(w_whole[b][:], w_rows[:, b, :])
-        w_piece = [
-            held.tile([P, KB_LAST, D_PIECE * P], BF16, name=f"w_piece{g}") for g in range(D // D_PIECE)
-        ]
-        for g in range(D // D_PIECE):
-            nc.sync.dma_start(
-                w_piece[g][:], w_rows[:, KB_STREAMED:, g * D_PIECE * P : (g + 1) * D_PIECE * P]
-            )
         offsets = held.tile([P, N // 16], U16, name="offsets")
         nc.sync.dma_start(offsets[:], offs)
         windows = [held.tile([P, S], F32, name=f"window{d}") for d in range(D)]
@@ -58,20 +48,15 @@ def tile_gemma4attention_kernel(tc, base, x, w, offs, out):
         nc.scalar.activation(one[:], one[:], ACT.Abs_reciprocal_sqrt)
 
         def multiply(b, d):
-            if b < KB_STREAMED:
-                weights = w_whole[b][:, d * P : (d + 1) * P]
-            else:
-                g, i = divmod(d, D_PIECE)
-                weights = w_piece[g][:, b - KB_STREAMED, i * P : (i + 1) * P]
+            weights = w_whole[b][:, d * P : (d + 1) * P]
             nc.tensor.matmul(raw[d][:], weights, x_sb[:, b, :], start=(b == 0), stop=(b == KB - 1))
 
-        for b in range(KB_STREAMED):
+        for b in range(KB - 1):
             for d in range(D):
                 multiply(b, d)
         sum_sq = [held.tile([P, N], F32, name=f"sum_sq{i}") for i in range(2)]
         for d in range(D):
-            for b in range(KB_STREAMED, KB):
-                multiply(b, d)
+            multiply(KB - 1, d)
             if d < 2:
                 nc.scalar.activation(sum_sq[d][:], raw[d][:], ACT.Square)
             else:

@@ -1,16 +1,21 @@
 import concourse.mybir as mybir
+from concourse.masks import make_identity
 
 BF16, F32, U16 = mybir.dt.bfloat16, mybir.dt.float32, mybir.dt.uint16
 ACT = mybir.ActivationFunctionType
 ALU = mybir.AluOpType
+AXIS = mybir.AxisListType
 
 P = 128
 C, S = 1024, 512
 K, N = 1024, 128
-D = C // P
+D = 8
+T = C // P
+HEADS = P // D
 KB = K // P
 EPS = 1e-6
 FLOPS = 2 * K * C * N
+KB_STREAMED = 5
 N_WARM = 18
 
 
@@ -18,57 +23,71 @@ def tile_gemma4attention_kernel(tc, base, x, w, offs, out):
     nc = tc.nc
     x_rows = x.rearrange("(p b) j -> p b j", b=KB)
     w_rows = w.rearrange("(p b) c -> p b c", b=KB)
-    base_blocks = base.rearrange("(d p) s -> d p s", p=P)
-    out_blocks = out.rearrange("(d p) s -> d p s", p=P)
+    base_tiles = base.rearrange("(m t) s -> t m s", t=T)
+    out_tiles = out.rearrange("(m t) s -> t m s", t=T)
 
     with (
         tc.tile_pool(name="held", bufs=1) as held,
         tc.psum_pool(name="psum", bufs=1) as psum,
+        tc.tile_pool(name="ring", bufs=2) as ring,
+        tc.tile_pool(name="ring_long", bufs=4) as ring_long,
+        tc.psum_pool(name="psum_ring", bufs=2) as psum_ring,
     ):
         x_sb = held.tile([P, KB, N], BF16, name="x_sb")
         nc.sync.dma_start(x_sb[:], x_rows)
-        w_whole = [held.tile([P, C], BF16, name=f"w_whole{b}") for b in range(KB)]
+        w_sb = [held.tile([P, P, T], BF16, name=f"w_sb{b}") for b in range(KB)]
         for b in range(KB):
-            nc.sync.dma_start(w_whole[b][:], w_rows[:, b, :])
+            nc.sync.dma_start(w_sb[b][:], w_rows[:, b, :].rearrange("p (m t) -> p m t", t=T))
         offsets = held.tile([P, N // 16], U16, name="offsets")
         nc.sync.dma_start(offsets[:], offs)
-        windows = [held.tile([P, S], F32, name=f"window{d}") for d in range(D)]
-        for d in range(D):
-            nc.sync.dma_start(windows[d][:], base_blocks[d])
+        windows = [held.tile([P, S], F32, name=f"window{t}") for t in range(T)]
+        for t in range(T):
+            nc.sync.dma_start(windows[t][:], base_tiles[t])
 
-        raw = [psum.tile([P, N], F32, name=f"raw{d}") for d in range(D)]
-        raw_sb = [held.tile([P, N], F32, name=f"raw_sb{d}") for d in range(D)]
+        raw_pair = [psum.tile([P, 2, N], F32, name=f"raw_pair{u}") for u in range(T // 2)]
 
         zeros = held.tile([P, N], BF16, name="zeros")
         nc.gpsimd.memset(zeros[:], 0.0)
         for i in range(N_WARM):
-            nc.tensor.matmul(raw[D - 1][:], zeros[:], zeros[:], start=True, stop=True)
+            nc.tensor.matmul(raw_pair[T // 2 - 1][:, 1, :], zeros[:], zeros[:], start=True, stop=True)
         one = held.tile([P, 1], F32, name="one")
         nc.vector.memset(one[:], 1.0)
         nc.scalar.activation(one[:], one[:], ACT.Abs_reciprocal_sqrt)
+        identity = held.tile([P, P], F32, name="identity")
+        make_identity(nc, identity[:])
+        folded = held.tile([P, HEADS], F32, name="folded")
+        nc.vector.tensor_reduce(
+            folded[:], identity[:].rearrange("p (g i) -> p i g", i=HEADS), axis=AXIS.X, op=ALU.add
+        )
+        same_head = held.tile([P, D, HEADS], F32, name="same_head")
+        nc.vector.tensor_copy(same_head[:], folded[:].unsqueeze(1).to_broadcast([P, D, HEADS]))
 
-        def multiply(b, d):
-            weights = w_whole[b][:, d * P : (d + 1) * P]
-            nc.tensor.matmul(raw[d][:], weights, x_sb[:, b, :], start=(b == 0), stop=(b == KB - 1))
+        def multiply(b, t):
+            nc.tensor.matmul(
+                raw_pair[t // 2][:, t % 2, :],
+                w_sb[b][:, :, t],
+                x_sb[:, b, :],
+                start=(b == 0 and t % 2 == 0),
+                stop=(b == KB - 1 and t % 2 == 1),
+            )
 
-        for b in range(KB - 1):
-            for d in range(D):
-                multiply(b, d)
-        sum_sq = [held.tile([P, N], F32, name=f"sum_sq{i}") for i in range(2)]
-        for d in range(D):
-            multiply(KB - 1, d)
-            if d < 2:
-                nc.scalar.activation(sum_sq[d][:], raw[d][:], ACT.Square)
-            else:
-                square = held.tile([P, N], F32, name=f"square{d}")
-                nc.scalar.activation(square[:], raw[d][:], ACT.Square)
-                nc.vector.tensor_add(sum_sq[d % 2][:], sum_sq[d % 2][:], square[:])
-            nc.vector.tensor_copy(raw_sb[d][:], raw[d][:])
-        nc.vector.tensor_add(sum_sq[0][:], sum_sq[0][:], sum_sq[1][:])
-        r = held.tile([P, N], F32, name="r")
-        nc.scalar.activation(r[:], sum_sq[0][:], ACT.Abs_reciprocal_sqrt, bias=EPS, scale=1.0 / D)
+        for b in range(KB_STREAMED):
+            for t in range(T):
+                multiply(b, t)
+        for u in range(T // 2):
+            for b in range(KB_STREAMED, KB):
+                multiply(b, 2 * u)
+                multiply(b, 2 * u + 1)
 
-        queues = (nc.scalar, nc.sync)
-        for d in range(D):
-            nc.vector.tensor_tensor(windows[d][:].indirect(offsets[:]), raw_sb[d][:], r[:], ALU.mult)
-            queues[d % 2].dma_start(out_blocks[d], windows[d][:])
+        for t in range(T):
+            raw = raw_pair[t // 2][:, t % 2, :]
+            square = ring.tile([P, N], F32, name="square")
+            nc.scalar.activation(square[:], raw, ACT.Square)
+            sum_sq = psum_ring.tile([P, N], F32, name="sum_sq")
+            nc.tensor.matmul(sum_sq[:], same_head[:].rearrange("p g i -> p (g i)"), square[:], start=True, stop=True)
+            r = ring_long.tile([P, N], F32, name="r")
+            nc.scalar.activation(r[:], sum_sq[:], ACT.Abs_reciprocal_sqrt, bias=EPS, scale=1.0 / D)
+            raw_sb = ring_long.tile([P, N], F32, name="raw_sb")
+            nc.scalar.copy(raw_sb[:], raw)
+            nc.vector.tensor_tensor(windows[t][:].indirect(offsets[:]), raw_sb[:], r[:], ALU.mult)
+            nc.sync.dma_start(out_tiles[t], windows[t][:])

@@ -15,7 +15,8 @@ HEADS = P // D
 KB = K // P
 EPS = 1e-6
 FLOPS = 2 * K * C * N
-KB_STREAMED = 5
+KB_LOAD = 2
+KB_STREAMED = 4
 N_WARM = 18
 
 
@@ -35,9 +36,12 @@ def tile_gemma4attention_kernel(tc, base, x, w, offs, out):
     ):
         x_sb = held.tile([P, KB, N], BF16, name="x_sb")
         nc.sync.dma_start(x_sb[:], x_rows)
-        w_sb = [held.tile([P, P, T], BF16, name=f"w_sb{b}") for b in range(KB)]
-        for b in range(KB):
-            nc.sync.dma_start(w_sb[b][:], w_rows[:, b, :].rearrange("p (m t) -> p m t", t=T))
+        w_sb = [held.tile([P, KB_LOAD, P, T], BF16, name=f"w_sb{g}") for g in range(KB // KB_LOAD)]
+        for g in range(KB // KB_LOAD):
+            nc.sync.dma_start(
+                w_sb[g][:],
+                w_rows[:, g * KB_LOAD : (g + 1) * KB_LOAD, :].rearrange("p b (m t) -> p b m t", t=T),
+            )
         offsets = held.tile([P, N // 16], U16, name="offsets")
         nc.sync.dma_start(offsets[:], offs)
         windows = [held.tile([P, S], F32, name=f"window{t}") for t in range(T)]
@@ -65,7 +69,7 @@ def tile_gemma4attention_kernel(tc, base, x, w, offs, out):
         def multiply(b, t):
             nc.tensor.matmul(
                 raw_pair[t // 2][:, t % 2, :],
-                w_sb[b][:, :, t],
+                w_sb[b // KB_LOAD][:, b % KB_LOAD, :, t],
                 x_sb[:, b, :],
                 start=(b == 0 and t % 2 == 0),
                 stop=(b == KB - 1 and t % 2 == 1),

import concourse.mybir as mybir
from concourse.masks import make_identity

BF16, F32, U16 = mybir.dt.bfloat16, mybir.dt.float32, mybir.dt.uint16
ACT = mybir.ActivationFunctionType
ALU = mybir.AluOpType
AXIS = mybir.AxisListType

P = 128
C, S = 1024, 512
K, N = 1024, 128
D = 8
T = C // P
HEADS = P // D
KB = K // P
EPS = 1e-6
FLOPS = 2 * K * C * N
KB_LOAD = 2
KB_STREAMED = 4
N_WARM = 18


def tile_gemma4attention_kernel(tc, base, x, w, offs, out):
    nc = tc.nc
    x_rows = x.rearrange("(p b) j -> p b j", b=KB)
    w_rows = w.rearrange("(p b) c -> p b c", b=KB)
    base_tiles = base.rearrange("(m t) s -> t m s", t=T)
    out_tiles = out.rearrange("(m t) s -> t m s", t=T)

    with (
        tc.tile_pool(name="held", bufs=1) as held,
        tc.psum_pool(name="psum", bufs=1) as psum,
        tc.tile_pool(name="ring", bufs=2) as ring,
        tc.tile_pool(name="ring_long", bufs=4) as ring_long,
        tc.psum_pool(name="psum_ring", bufs=2) as psum_ring,
    ):
        x_sb = held.tile([P, KB, N], BF16, name="x_sb")
        nc.sync.dma_start(x_sb[:], x_rows)
        w_sb = [held.tile([P, KB_LOAD, P, T], BF16, name=f"w_sb{g}") for g in range(KB // KB_LOAD)]
        for g in range(KB // KB_LOAD):
            nc.sync.dma_start(
                w_sb[g][:],
                w_rows[:, g * KB_LOAD : (g + 1) * KB_LOAD, :].rearrange("p b (m t) -> p b m t", t=T),
            )
        offsets = held.tile([P, N // 16], U16, name="offsets")
        nc.sync.dma_start(offsets[:], offs)
        windows = [held.tile([P, S], F32, name=f"window{t}") for t in range(T)]
        for t in range(T):
            nc.sync.dma_start(windows[t][:], base_tiles[t])

        raw_pair = [psum.tile([P, 2, N], F32, name=f"raw_pair{u}") for u in range(T // 2)]

        zeros = held.tile([P, N], BF16, name="zeros")
        nc.gpsimd.memset(zeros[:], 0.0)
        for i in range(N_WARM):
            nc.tensor.matmul(raw_pair[T // 2 - 1][:, 1, :], zeros[:], zeros[:], start=True, stop=True)
        one = held.tile([P, 1], F32, name="one")
        nc.vector.memset(one[:], 1.0)
        nc.scalar.activation(one[:], one[:], ACT.Abs_reciprocal_sqrt)
        identity = held.tile([P, P], F32, name="identity")
        make_identity(nc, identity[:])
        folded = held.tile([P, HEADS], F32, name="folded")
        nc.vector.tensor_reduce(
            folded[:], identity[:].rearrange("p (g i) -> p i g", i=HEADS), axis=AXIS.X, op=ALU.add
        )
        same_head = held.tile([P, D, HEADS], F32, name="same_head")
        nc.vector.tensor_copy(same_head[:], folded[:].unsqueeze(1).to_broadcast([P, D, HEADS]))

        def multiply(b, t):
            nc.tensor.matmul(
                raw_pair[t // 2][:, t % 2, :],
                w_sb[b // KB_LOAD][:, b % KB_LOAD, :, t],
                x_sb[:, b, :],
                start=(b == 0 and t % 2 == 0),
                stop=(b == KB - 1 and t % 2 == 1),
            )

        for b in range(KB_STREAMED):
            for t in range(T):
                multiply(b, t)
        for u in range(T // 2):
            for b in range(KB_STREAMED, KB):
                multiply(b, 2 * u)
                multiply(b, 2 * u + 1)

        for t in range(T):
            raw = raw_pair[t // 2][:, t % 2, :]
            square = ring.tile([P, N], F32, name="square")
            nc.scalar.activation(square[:], raw, ACT.Square)
            sum_sq = psum_ring.tile([P, N], F32, name="sum_sq")
            nc.tensor.matmul(sum_sq[:], same_head[:].rearrange("p g i -> p (g i)"), square[:], start=True, stop=True)
            r = ring_long.tile([P, N], F32, name="r")
            nc.scalar.activation(r[:], sum_sq[:], ACT.Abs_reciprocal_sqrt, bias=EPS, scale=1.0 / D)
            raw_sb = ring_long.tile([P, N], F32, name="raw_sb")
            nc.scalar.copy(raw_sb[:], raw)
            nc.vector.tensor_tensor(windows[t][:].indirect(offsets[:]), raw_sb[:], r[:], ALU.mult)
            nc.sync.dma_start(out_tiles[t], windows[t][:])
